import numpy as np
import ml_dtypes


def mxq(x, axis, fmt="e4m3"):
    dtype, down = {"e4m3": (ml_dtypes.float8_e4m3fn, 7), "e5m2": (ml_dtypes.float8_e5m2, 14)}[fmt]
    v = np.moveaxis(np.asarray(x, np.float32).astype(ml_dtypes.bfloat16).astype(np.float64), axis, -1)
    blocks = v.reshape(v.shape[:-1] + (-1, 32))
    amax = np.abs(blocks).max(-1, keepdims=True)
    byte = np.maximum(np.where(amax > 0, np.frexp(amax)[1] - 1 + 127, 0) - down, 1)
    scale = np.exp2(byte - 127.0)
    codes = (blocks / scale).astype(np.float32).astype(dtype).astype(np.float64)
    return np.moveaxis((codes * scale).reshape(v.shape), -1, axis)


WIDE = False


def mx_kscale(k):
    if not WIDE:
        return np.ones(k)
    levels = np.array([10, -10, 5, -5, 0])
    if k % 512:
        return np.exp2(np.random.permutation(np.resize(levels, k // 32))).repeat(32)
    a = np.empty((k // 512, 16))
    for p in range(k // 512):
        a[p, :8] = np.random.permutation(np.resize(levels, 8))
        for g in range(8):
            far = levels[np.abs(levels - a[p, g]) >= 10]
            a[p, g + 8] = far[np.random.randint(len(far))]
    return np.exp2(a.ravel()).repeat(32)


BF16 = ml_dtypes.bfloat16


def bf(x):
    return np.asarray(x, np.float32).astype(BF16)


def f64(x):
    return np.asarray(x).astype(np.float64)


B, K, D, H1, H2, C = 4096, 2, 1024, 512, 128, 64


def setup_inputs():
    s, t = mx_kscale(D), mx_kscale(H1)
    return {"nf0": bf(np.random.standard_normal((B, D)) * s),
            "nf1": bf(np.random.standard_normal((B * K, D)) * s),
            "a1": bf(np.maximum(np.random.standard_normal((B * K, H1)) * np.sqrt(1.0 + 1.0 / K), 0.0) * t),
            "w1_0": bf(np.random.standard_normal((D, H1)) / np.sqrt(D) / s[:, None] * t),
            "w2_0": bf(np.random.standard_normal((D, H1)) / np.sqrt(D) / s[:, None] * t),
            "w1_1": bf(np.random.standard_normal((H1, H2)) / np.sqrt(H1) / t[:, None]),
            "w2_1": bf(np.random.standard_normal((H1, H2)) / np.sqrt(H1) / t[:, None])}


def sage_gcn(cur, neigh, w1, w2):
    b, d = cur.shape
    agg = neigh.reshape(b, -1, d).mean(axis=1)
    return np.maximum((mxq(cur, 1, "e4m3") @ mxq(w2, 0, "e4m3")) + (mxq(agg, 1, "e4m3") @ mxq(w1, 0, "e4m3")), 0.0)


def reference(nf0, nf1, a1, w1_0, w2_0, w1_1, w2_1):
    a0 = sage_gcn(f64(nf0), f64(nf1), f64(w1_0), f64(w2_0))
    return sage_gcn(a0, f64(a1), f64(w1_1), f64(w2_1))

@@ -1,0 +1,275 @@
+from contextlib import ExitStack
+
+import concourse.mybir as mybir
+from concourse.masks import make_identity
+
+F32 = mybir.dt.float32
+BF16 = mybir.dt.bfloat16
+U32 = mybir.dt.uint32
+U8 = mybir.dt.uint8
+FP8X4 = mybir.dt.float8_e4m3fn_x4
+ACT = mybir.ActivationFunctionType
+ALU = mybir.AluOpType
+
+P = 128
+PACK = 4
+K_PASS = P * PACK
+B, D, H1, H2 = 4096, 1024, 512, 128
+FLOPS = 2 * B * (2 * D * H1 + 2 * H1 * H2)
+
+PAIRS = B // (2 * P)
+PAIR = 2 * P
+L1_PASSES = 2 * D // K_PASS
+AHEAD = 5
+SLICES_PER_BANK = 4
+
+
+def tile_graphsage_pb_t_kernel(tc, nf0, nf1, a1, w1_0, w2_0, w1_1, w2_1, out):
+    nc = tc.nc
+    with ExitStack() as ctx:
+        const = ctx.enter_context(tc.tile_pool(name="const", bufs=1))
+        weights_in = ctx.enter_context(tc.tile_pool(name="weights_in", bufs=L1_PASSES))
+        weights_grouped = ctx.enter_context(tc.tile_pool(name="weights_grouped", bufs=L1_PASSES))
+        loads = ctx.enter_context(tc.tile_pool(name="loads", bufs=AHEAD + 1))
+        sums = ctx.enter_context(tc.tile_pool(name="sums", bufs=3))
+        grouped = ctx.enter_context(tc.tile_pool(name="grouped", bufs=2))
+        codes = ctx.enter_context(tc.tile_pool(name="codes", bufs=3))
+        results = ctx.enter_context(tc.tile_pool(name="results", bufs=4))
+        psum = ctx.enter_context(tc.psum_pool(name="psum", bufs=1))
+        ctx.enter_context(tc.manual_schedule())
+
+        nf0_rows = nf0.rearrange("(p x) k -> p (x k)", p=P)
+        nf1_rows = nf1.rearrange("(p x) k -> p (x k)", p=P)
+        a1_rows = a1.rearrange("(p x) k -> p (x k)", p=P)
+        out_rows = out.rearrange("(p x) c -> p (x c)", p=P)
+
+        identity_f32 = const.tile([P, P], F32, name="identity_f32")
+        make_identity(nc, identity_f32[:])
+
+        w_l1_codes = const.tile([P, L1_PASSES, H1], U32, name="w_l1_codes", align_bytes=64)
+        w_l1_scales = const.tile([P, L1_PASSES, H1], U8, name="w_l1_scales", align_bytes=64)
+        w_l2_codes = const.tile([P, 2, H2], U32, name="w_l2_codes", align_bytes=64)
+        w_l2_scales = const.tile([P, 2, H2], U8, name="w_l2_scales", align_bytes=64)
+
+        held = {}
+
+
+        def load_layer1_weights():
+            for c in range(L1_PASSES):
+                raw = weights_in.tile([P, PACK, H1], BF16, name="w_l1_raw", tag="w_l1_raw")
+                w = w2_0 if c < 2 else w1_0
+                rows = w[K_PASS * (c % 2) : K_PASS * (c % 2 + 1), :]
+                nc.sync.dma_start(out=raw[:], in_=rows.rearrange("(p t) h -> p t h", t=PACK))
+                held[("w_raw", c)] = raw
+
+        def load_layer2_weights():
+            for c, w in enumerate((w2_1, w1_1)):
+                raw = weights_in.tile([P, PACK, H2], BF16, name="w_l2_raw", tag="w_l2_raw", bufs=2)
+                nc.sync.dma_start(out=raw[:], in_=w.rearrange("(p t) c -> p t c", t=PACK))
+                held[("w_raw", L1_PASSES + c)] = raw
+
+        def group_weights(c, engine_copy):
+            width = H1 if c < L1_PASSES else H2
+            side_by_side = weights_grouped.tile(
+                [P, width, PACK], BF16, name="w_grouped", tag="w_grouped_%d" % width, align_bytes=64
+            )
+            if c < L1_PASSES:
+                engine_copy(
+                    out=side_by_side[:].rearrange("p (q m) t -> p q m t", q=PACK),
+                    in_=held[("w_raw", c)][:].rearrange("p t (m q) -> p q m t", q=PACK),
+                )
+            else:
+                engine_copy(
+                    out=side_by_side[:].rearrange("p (c i) t -> p c t i", i=4),
+                    in_=held[("w_raw", c)][:].rearrange("p t (c i) -> p c t i", i=4),
+                )
+            held[("w_grouped", c)] = side_by_side
+
+        def quantise_weights(c):
+            values = held[("w_grouped", c)][:].rearrange("p h t -> p (h t)")
+            if c < L1_PASSES:
+                words, scales = w_l1_codes[:, c, :], w_l1_scales[:, c, :]
+            else:
+                words, scales = w_l2_codes[:, c - L1_PASSES, :], w_l2_scales[:, c - L1_PASSES, :]
+            nc.vector.quantize_mx(out=words.bitcast(FP8X4), scales=scales, in_=values)
+
+
+        def load_pair(n):
+            nf1_in = loads.tile([P, 4 * D], BF16, name="nf1_in", tag="nf1_in")
+            nc.sync.dma_start(out=nf1_in[:], in_=nf1_rows[:, 4 * D * n : 4 * D * (n + 1)])
+            a1_in = loads.tile([P, 4 * H1], BF16, name="a1_in", tag="a1_in")
+            nc.sync.dma_start(out=a1_in[:], in_=a1_rows[:, 4 * H1 * n : 4 * H1 * (n + 1)])
+            nf0_in = loads.tile([P, 2 * D], BF16, name="nf0_in", tag="nf0_in")
+            nc.sync.dma_start(out=nf0_in[:], in_=nf0_rows[:, 2 * D * n : 2 * D * (n + 1)])
+            held[("nf1", n)], held[("a1", n)], held[("nf0", n)] = nf1_in, a1_in, nf0_in
+
+        def add_neighbours(n):
+            mean = sums.tile([P, 2 * D + 2 * H1], BF16, name="mean", tag="mean")
+            for kind, width, start in (("nf1", D, 0), ("a1", H1, 2 * D)):
+                rows = held[(kind, n)][:].rearrange("p (j s k) -> p j s k", j=2, s=2)
+                nc.vector.tensor_tensor(
+                    out=mean[:, start : start + 2 * width].rearrange("p (j k) -> p j k", j=2),
+                    in0=rows[:, :, 0, :],
+                    in1=rows[:, :, 1, :],
+                    op=ALU.add,
+                )
+            nc.vector.tensor_scalar_mul(out=mean[:], in0=mean[:], scalar1=0.5)
+            held[("mean", n)] = mean
+
+        def transpose_pair(n):
+            mean_words = held[("mean", n)][:].bitcast(F32)
+            for j in range(2):
+                agg0_t = psum.tile([P, 2, 2, P], F32, name="agg0_t%d" % j, tag="agg0_t%d" % j)
+                for g in range(2):
+                    for u in range(2):
+                        w0 = (D // 2) * j + (K_PASS // 2) * g
+                        nc.tensor.transpose(agg0_t[:, g, u, :], mean_words[:, w0 + u : w0 + 2 * P : 2], identity_f32[:])
+                held[("agg0_t", n, j)] = agg0_t
+            agg1_t = psum.tile([P, 2, 2, P], F32, name="agg1_t", tag="agg1_t")
+            for j in range(2):
+                for u in range(2):
+                    w0 = D + (H1 // 2) * j
+                    nc.tensor.transpose(agg1_t[:, j, u, :], mean_words[:, w0 + u : w0 + 2 * P : 2], identity_f32[:])
+            held[("agg1_t", n)] = agg1_t
+            nf0_words = held[("nf0", n)][:].bitcast(F32)
+            for j in range(2):
+                nf0_t = psum.tile([P, 2, 2, P], F32, name="nf0_t%d" % j, tag="nf0_t%d" % j)
+                for g in range(2):
+                    for u in range(2):
+                        w0 = (D // 2) * j + (K_PASS // 2) * g
+                        nc.tensor.transpose(nf0_t[:, g, u, :], nf0_words[:, w0 + u : w0 + 2 * P : 2], identity_f32[:])
+                held[("nf0_t", n, j)] = nf0_t
+
+        def copy_out(n):
+            x_grouped = grouped.tile([P, L1_PASSES * PAIR * PACK], BF16, name="x_grouped", tag="x_grouped", align_bytes=64)
+            as_words = x_grouped[:].bitcast(F32).rearrange("p (c j b u) -> p j c b u", c=L1_PASSES, j=2, b=P, u=2)
+            for j in range(2):
+                nc.scalar.copy(
+                    out=as_words[:, j, 2:4, :, :],
+                    in_=held[("agg0_t", n, j)][:].rearrange("p g u b -> p g b u"),
+                )
+            agg1_grouped = grouped.tile([P, PAIR * PACK], BF16, name="agg1_grouped", tag="agg1_grouped", align_bytes=64)
+            nc.scalar.copy(
+                out=agg1_grouped[:].bitcast(F32).rearrange("p (j b u) -> p j b u", j=2, b=P, u=2),
+                in_=held[("agg1_t", n)][:].rearrange("p j u b -> p j b u"),
+            )
+            for j in range(2):
+                nc.scalar.copy(
+                    out=as_words[:, j, 0:2, :, :],
+                    in_=held[("nf0_t", n, j)][:].rearrange("p g u b -> p g b u"),
+                )
+            held[("x_grouped", n)], held[("agg1_grouped", n)] = x_grouped, agg1_grouped
+
+        def quantise_pair(n):
+            x_codes = codes.tile([P, L1_PASSES * PAIR], U32, name="x_codes", tag="x_codes", align_bytes=64)
+            x_scales = codes.tile([P, L1_PASSES * PAIR], U8, name="x_scales", tag="x_scales", align_bytes=64)
+            agg1_codes = codes.tile([P, PAIR], U32, name="agg1_codes", tag="agg1_codes", align_bytes=64)
+            agg1_scales = codes.tile([P, PAIR], U8, name="agg1_scales", tag="agg1_scales", align_bytes=64)
+            for half in (1, 0):
+                cols = slice(2 * PAIR * half, 2 * PAIR * (half + 1))
+                nc.vector.quantize_mx(
+                    out=x_codes[:, cols].bitcast(FP8X4),
+                    scales=x_scales[:, cols],
+                    in_=held[("x_grouped", n)][:, 2 * PAIR * PACK * half : 2 * PAIR * PACK * (half + 1)],
+                )
+                if half == 1:
+                    nc.vector.quantize_mx(
+                        out=agg1_codes[:].bitcast(FP8X4), scales=agg1_scales[:], in_=held[("agg1_grouped", n)][:]
+                    )
+            held[("x_codes", n)], held[("x_scales", n)] = x_codes, x_scales
+            held[("agg1_codes", n)], held[("agg1_scales", n)] = agg1_codes, agg1_scales
+
+
+        def layer1(n):
+            x_codes, x_scales = held[("x_codes", n)], held[("x_scales", n)]
+            a0_grouped = grouped.tile([P, PAIR * PACK], BF16, name="a0_grouped", tag="a0_grouped", align_bytes=64)
+            by_bank = a0_grouped[:].rearrange("p (b h t) -> p h b t", b=PAIR, h=2, t=2)
+            for h in range(2):
+                a0_t = psum.tile([P, 2, PAIR], F32, name="a0_t%d" % h, tag="a0_t%d" % h)
+                for t in range(2):
+                    hidden = slice(P * (2 * h + t), P * (2 * h + t + 1))
+                    for c in range(L1_PASSES):
+                        roots = slice(PAIR * c, PAIR * (c + 1))
+                        nc.tensor.matmul_mx(
+                            out=a0_t[:, t, :],
+                            lhsT=w_l1_codes[:, c, hidden].bitcast(FP8X4),
+                            lhsT_scale=w_l1_scales[:, c, hidden],
+                            rhs=x_codes[:, roots].bitcast(FP8X4),
+                            rhs_scale=x_scales[:, roots],
+                            start=(c == 0),
+                            stop=(c == L1_PASSES - 1),
+                        )
+                nc.scalar.activation(out=by_bank[:, h, :, :], in_=a0_t[:].rearrange("p t b -> p b t"), func=ACT.Relu)
+            held[("a0_grouped", n)] = a0_grouped
+
+        def quantise_hidden(n):
+            a0_codes = codes.tile([P, PAIR], U32, name="a0_codes", tag="a0_codes", align_bytes=64)
+            a0_scales = codes.tile([P, PAIR], U8, name="a0_scales", tag="a0_scales", align_bytes=64)
+            nc.vector.quantize_mx(out=a0_codes[:].bitcast(FP8X4), scales=a0_scales[:], in_=held[("a0_grouped", n)][:])
+            held[("a0_codes", n)], held[("a0_scales", n)] = a0_codes, a0_scales
+
+        def layer2(n):
+            for j in range(2):
+                x = 2 * n + j
+                place = x % SLICES_PER_BANK
+                if place == 0:
+                    held["out_bank"] = psum.tile([P, SLICES_PER_BANK, H2], F32, name="out_bank", tag="out_bank")
+                out_bank = held["out_bank"]
+                roots = slice(P * j, P * (j + 1))
+                for c, kind in enumerate(("a0", "agg1")):
+                    nc.tensor.matmul_mx(
+                        out=out_bank[:, place, :],
+                        lhsT=held[(kind + "_codes", n)][:, roots].bitcast(FP8X4),
+                        lhsT_scale=held[(kind + "_scales", n)][:, roots],
+                        rhs=w_l2_codes[:, c, :].bitcast(FP8X4),
+                        rhs_scale=w_l2_scales[:, c, :],
+                        start=(c == 0),
+                        stop=(c == 1),
+                    )
+            count = 2 if n >= PAIRS - 2 else SLICES_PER_BANK
+            last = 2 * n + 1
+            if (last + 1) % count == 0:
+                first = last + 1 - count
+                result = results.tile([P, count, H2], F32, name="result", tag="result")
+                nc.vector.tensor_relu(
+                    out=result[:], in_=held["out_bank"][:, first % SLICES_PER_BANK : first % SLICES_PER_BANK + count, :]
+                )
+                nc.sync.dma_start(
+                    out=out_rows[:, H2 * first : H2 * (first + count)], in_=result[:].rearrange("p s c -> p (s c)")
+                )
+
+
+        load_layer1_weights()
+        load_pair(0)
+        load_pair(1)
+        load_layer2_weights()
+        for n in range(2, AHEAD):
+            load_pair(n)
+
+        for c in range(L1_PASSES):
+            group_weights(c, nc.vector.tensor_copy if c % 2 == 0 else nc.scalar.copy)
+        for c in range(L1_PASSES - 1):
+            quantise_weights(c)
+        add_neighbours(0)
+        quantise_weights(L1_PASSES - 1)
+
+        for i in range(PAIRS + 2):
+            if i + AHEAD < PAIRS:
+                load_pair(i + AHEAD)
+            if i >= 2:
+                quantise_hidden(i - 2)
+            if i + 1 < PAIRS:
+                add_neighbours(i + 1)
+            if i < PAIRS:
+                transpose_pair(i)
+                copy_out(i)
+                quantise_pair(i)
+            if i == 0:
+                group_weights(4, nc.vector.tensor_copy)
+                group_weights(5, nc.vector.tensor_copy)
+                quantise_weights(4)
+                quantise_weights(5)
+            if 1 <= i <= PAIRS:
+                layer1(i - 1)
+            if i >= 2:
+                layer2(i - 2)

@@ -20,6 +20,8 @@ FLOPS = 2 * B * (2 * D * H1 + 2 * H1 * H2)
 PAIRS = B // (2 * P)
 PAIR = 2 * P
 L1_PASSES = 2 * D // K_PASS
+NEIGHBOUR_WEIGHTS = (2, 3, L1_PASSES + 1)
+WEIGHT_ORDER = (2, 0, 3, 1)
 AHEAD = 5
 SLICES_PER_BANK = 4
 
@@ -55,7 +57,7 @@ def tile_graphsage_pb_t_kernel(tc, nf0, nf1, a1, w1_0, w2_0, w1_1, w2_1, out):
 
 
         def load_layer1_weights():
-            for c in range(L1_PASSES):
+            for c in WEIGHT_ORDER:
                 raw = weights_in.tile([P, PACK, H1], BF16, name="w_l1_raw", tag="w_l1_raw")
                 w = w2_0 if c < 2 else w1_0
                 rows = w[K_PASS * (c % 2) : K_PASS * (c % 2 + 1), :]
@@ -68,7 +70,13 @@ def tile_graphsage_pb_t_kernel(tc, nf0, nf1, a1, w1_0, w2_0, w1_1, w2_1, out):
                 nc.sync.dma_start(out=raw[:], in_=w.rearrange("(p t) c -> p t c", t=PACK))
                 held[("w_raw", L1_PASSES + c)] = raw
 
-        def group_weights(c, engine_copy):
+        def group_weights(c):
+            if c in NEIGHBOUR_WEIGHTS:
+                engine_copy = lambda out, in_: nc.vector.tensor_scalar_mul(out=out, in0=in_, scalar1=0.5)
+            elif c < L1_PASSES:
+                engine_copy = nc.scalar.copy
+            else:
+                engine_copy = nc.vector.tensor_copy
             width = H1 if c < L1_PASSES else H2
             side_by_side = weights_grouped.tile(
                 [P, width, PACK], BF16, name="w_grouped", tag="w_grouped_%d" % width, align_bytes=64
@@ -104,32 +112,34 @@ def tile_graphsage_pb_t_kernel(tc, nf0, nf1, a1, w1_0, w2_0, w1_1, w2_1, out):
             held[("nf1", n)], held[("a1", n)], held[("nf0", n)] = nf1_in, a1_in, nf0_in
 
         def add_neighbours(n):
-            mean = sums.tile([P, 2 * D + 2 * H1], BF16, name="mean", tag="mean")
+            total = sums.tile([P, 2 * D + 2 * H1], BF16, name="total", tag="total")
             for kind, width, start in (("nf1", D, 0), ("a1", H1, 2 * D)):
-                rows = held[(kind, n)][:].rearrange("p (j s k) -> p j s k", j=2, s=2)
-                nc.vector.tensor_tensor(
-                    out=mean[:, start : start + 2 * width].rearrange("p (j k) -> p j k", j=2),
-                    in0=rows[:, :, 0, :],
-                    in1=rows[:, :, 1, :],
-                    op=ALU.add,
-                )
-            nc.vector.tensor_scalar_mul(out=mean[:], in0=mean[:], scalar1=0.5)
-            held[("mean", n)] = mean
+                rows = held[(kind, n)][:].rearrange("p (j s w u e) -> p j s u w e", j=2, s=2, u=2, e=2)
+                for j in range(2):
+                    nc.vector.tensor_tensor(
+                        out=total[:, start + width * j : start + width * (j + 1)].rearrange(
+                            "p (u w e) -> p u w e", u=2, e=2
+                        ),
+                        in0=rows[:, j, 0],
+                        in1=rows[:, j, 1],
+                        op=ALU.add,
+                    )
+            held[("sum", n)] = total
 
         def transpose_pair(n):
-            mean_words = held[("mean", n)][:].bitcast(F32)
+            sum_words = held[("sum", n)][:].bitcast(F32)
             for j in range(2):
                 agg0_t = psum.tile([P, 2, 2, P], F32, name="agg0_t%d" % j, tag="agg0_t%d" % j)
                 for g in range(2):
                     for u in range(2):
-                        w0 = (D // 2) * j + (K_PASS // 2) * g
-                        nc.tensor.transpose(agg0_t[:, g, u, :], mean_words[:, w0 + u : w0 + 2 * P : 2], identity_f32[:])
+                        w0 = (D // 2) * j + (D // 4) * u + P * g
+                        nc.tensor.transpose(agg0_t[:, g, u, :], sum_words[:, w0 : w0 + P], identity_f32[:])
                 held[("agg0_t", n, j)] = agg0_t
             agg1_t = psum.tile([P, 2, 2, P], F32, name="agg1_t", tag="agg1_t")
             for j in range(2):
                 for u in range(2):
-                    w0 = D + (H1 // 2) * j
-                    nc.tensor.transpose(agg1_t[:, j, u, :], mean_words[:, w0 + u : w0 + 2 * P : 2], identity_f32[:])
+                    w0 = D + (H1 // 2) * j + P * u
+                    nc.tensor.transpose(agg1_t[:, j, u, :], sum_words[:, w0 : w0 + P], identity_f32[:])
             held[("agg1_t", n)] = agg1_t
             nf0_words = held[("nf0", n)][:].bitcast(F32)
             for j in range(2):
@@ -246,12 +256,12 @@ def tile_graphsage_pb_t_kernel(tc, nf0, nf1, a1, w1_0, w2_0, w1_1, w2_1, out):
         for n in range(2, AHEAD):
             load_pair(n)
 
-        for c in range(L1_PASSES):
-            group_weights(c, nc.vector.tensor_copy if c % 2 == 0 else nc.scalar.copy)
-        for c in range(L1_PASSES - 1):
+        for c in WEIGHT_ORDER:
+            group_weights(c)
+        for c in WEIGHT_ORDER[:-1]:
             quantise_weights(c)
         add_neighbours(0)
-        quantise_weights(L1_PASSES - 1)
+        quantise_weights(WEIGHT_ORDER[-1])
 
         for i in range(PAIRS + 2):
             if i + AHEAD < PAIRS:
@@ -265,8 +275,8 @@ def tile_graphsage_pb_t_kernel(tc, nf0, nf1, a1, w1_0, w2_0, w1_1, w2_1, out):
                 copy_out(i)
                 quantise_pair(i)
             if i == 0:
-                group_weights(4, nc.vector.tensor_copy)
-                group_weights(5, nc.vector.tensor_copy)
+                group_weights(4)
+                group_weights(5)
                 quantise_weights(4)
                 quantise_weights(5)
             if 1 <= i <= PAIRS:

@@ -126,6 +126,14 @@ def tile_graphsage_pb_t_kernel(tc, nf0, nf1, a1, w1_0, w2_0, w1_1, w2_1, out):
                     )
             held[("sum", n)] = total
 
+        def order_roots(n):
+            ordered = sums.tile([P, D], F32, name="ordered", tag="ordered", bufs=2)
+            nc.vector.tensor_copy(
+                out=ordered[:].rearrange("p (j u w) -> p j u w", j=2, u=2),
+                in_=held[("nf0", n)][:].bitcast(F32).rearrange("p (j w u) -> p j u w", j=2, u=2),
+            )
+            held[("ordered", n)] = ordered
+
         def transpose_pair(n):
             sum_words = held[("sum", n)][:].bitcast(F32)
             for j in range(2):
@@ -141,13 +149,13 @@ def tile_graphsage_pb_t_kernel(tc, nf0, nf1, a1, w1_0, w2_0, w1_1, w2_1, out):
                     w0 = D + (H1 // 2) * j + P * u
                     nc.tensor.transpose(agg1_t[:, j, u, :], sum_words[:, w0 : w0 + P], identity_f32[:])
             held[("agg1_t", n)] = agg1_t
-            nf0_words = held[("nf0", n)][:].bitcast(F32)
+            ordered = held[("ordered", n)]
             for j in range(2):
                 nf0_t = psum.tile([P, 2, 2, P], F32, name="nf0_t%d" % j, tag="nf0_t%d" % j)
                 for g in range(2):
                     for u in range(2):
-                        w0 = (D // 2) * j + (K_PASS // 2) * g
-                        nc.tensor.transpose(nf0_t[:, g, u, :], nf0_words[:, w0 + u : w0 + 2 * P : 2], identity_f32[:])
+                        w0 = (D // 2) * j + (D // 4) * u + P * g
+                        nc.tensor.transpose(nf0_t[:, g, u, :], ordered[:, w0 : w0 + P], identity_f32[:])
                 held[("nf0_t", n, j)] = nf0_t
 
         def copy_out(n):
@@ -261,6 +269,7 @@ def tile_graphsage_pb_t_kernel(tc, nf0, nf1, a1, w1_0, w2_0, w1_1, w2_1, out):
         for c in WEIGHT_ORDER[:-1]:
             quantise_weights(c)
         add_neighbours(0)
+        order_roots(0)
         quantise_weights(WEIGHT_ORDER[-1])
 
         for i in range(PAIRS + 2):
@@ -270,6 +279,7 @@ def tile_graphsage_pb_t_kernel(tc, nf0, nf1, a1, w1_0, w2_0, w1_1, w2_1, out):
                 quantise_hidden(i - 2)
             if i + 1 < PAIRS:
                 add_neighbours(i + 1)
+                order_roots(i + 1)
             if i < PAIRS:
                 transpose_pair(i)
                 copy_out(i)

@@ -201,13 +201,12 @@ def tile_graphsage_pb_t_kernel(tc, nf0, nf1, a1, w1_0, w2_0, w1_1, w2_1, out):
         def layer1(n):
             x_codes, x_scales = held[("x_codes", n)], held[("x_scales", n)]
             a0_grouped = grouped.tile([P, PAIR * PACK], BF16, name="a0_grouped", tag="a0_grouped", align_bytes=64)
-            by_bank = a0_grouped[:].rearrange("p (b h t) -> p h b t", b=PAIR, h=2, t=2)
-            for h in range(2):
-                a0_t = psum.tile([P, 2, PAIR], F32, name="a0_t%d" % h, tag="a0_t%d" % h)
-                for t in range(2):
-                    hidden = slice(P * (2 * h + t), P * (2 * h + t + 1))
+            for j in range(2):
+                a0_t = psum.tile([P, PACK, P], F32, name="a0_t%d" % j, tag="a0_t%d" % j)
+                for t in range(PACK):
+                    hidden = slice(P * t, P * (t + 1))
                     for c in range(L1_PASSES):
-                        roots = slice(PAIR * c, PAIR * (c + 1))
+                        roots = slice(PAIR * c + P * j, PAIR * c + P * (j + 1))
                         nc.tensor.matmul_mx(
                             out=a0_t[:, t, :],
                             lhsT=w_l1_codes[:, c, hidden].bitcast(FP8X4),
@@ -217,7 +216,11 @@ def tile_graphsage_pb_t_kernel(tc, nf0, nf1, a1, w1_0, w2_0, w1_1, w2_1, out):
                             start=(c == 0),
                             stop=(c == L1_PASSES - 1),
                         )
-                nc.scalar.activation(out=by_bank[:, h, :, :], in_=a0_t[:].rearrange("p t b -> p b t"), func=ACT.Relu)
+                nc.scalar.activation(
+                    out=a0_grouped[:, P * PACK * j : P * PACK * (j + 1)].rearrange("p (b t) -> p b t", t=PACK),
+                    in_=a0_t[:].rearrange("p t b -> p b t"),
+                    func=ACT.Relu,
+                )
             held[("a0_grouped", n)] = a0_grouped
 
         def quantise_hidden(n):

@@ -166,9 +166,11 @@ def tile_graphsage_pb_t_kernel(tc, nf0, nf1, a1, w1_0, w2_0, w1_1, w2_1, out):
                     out=as_words[:, j, 2:4, :, :],
                     in_=held[("agg0_t", n, j)][:].rearrange("p g u b -> p g b u"),
                 )
-            agg1_grouped = grouped.tile([P, PAIR * PACK], BF16, name="agg1_grouped", tag="agg1_grouped", align_bytes=64)
+            y_grouped = grouped.tile(
+                [P, 2 * PAIR * PACK], BF16, name="y_grouped", tag="y_grouped", align_bytes=64, bufs=3
+            )
             nc.scalar.copy(
-                out=agg1_grouped[:].bitcast(F32).rearrange("p (j b u) -> p j b u", j=2, b=P, u=2),
+                out=y_grouped[:, PAIR * PACK :].bitcast(F32).rearrange("p (j b u) -> p j b u", j=2, b=P, u=2),
                 in_=held[("agg1_t", n)][:].rearrange("p j u b -> p j b u"),
             )
             for j in range(2):
@@ -176,13 +178,11 @@ def tile_graphsage_pb_t_kernel(tc, nf0, nf1, a1, w1_0, w2_0, w1_1, w2_1, out):
                     out=as_words[:, j, 0:2, :, :],
                     in_=held[("nf0_t", n, j)][:].rearrange("p g u b -> p g b u"),
                 )
-            held[("x_grouped", n)], held[("agg1_grouped", n)] = x_grouped, agg1_grouped
+            held[("x_grouped", n)], held[("y_grouped", n)] = x_grouped, y_grouped
 
         def quantise_pair(n):
             x_codes = codes.tile([P, L1_PASSES * PAIR], U32, name="x_codes", tag="x_codes", align_bytes=64)
             x_scales = codes.tile([P, L1_PASSES * PAIR], U8, name="x_scales", tag="x_scales", align_bytes=64)
-            agg1_codes = codes.tile([P, PAIR], U32, name="agg1_codes", tag="agg1_codes", align_bytes=64)
-            agg1_scales = codes.tile([P, PAIR], U8, name="agg1_scales", tag="agg1_scales", align_bytes=64)
             for half in (1, 0):
                 cols = slice(2 * PAIR * half, 2 * PAIR * (half + 1))
                 nc.vector.quantize_mx(
@@ -190,17 +190,12 @@ def tile_graphsage_pb_t_kernel(tc, nf0, nf1, a1, w1_0, w2_0, w1_1, w2_1, out):
                     scales=x_scales[:, cols],
                     in_=held[("x_grouped", n)][:, 2 * PAIR * PACK * half : 2 * PAIR * PACK * (half + 1)],
                 )
-                if half == 1:
-                    nc.vector.quantize_mx(
-                        out=agg1_codes[:].bitcast(FP8X4), scales=agg1_scales[:], in_=held[("agg1_grouped", n)][:]
-                    )
             held[("x_codes", n)], held[("x_scales", n)] = x_codes, x_scales
-            held[("agg1_codes", n)], held[("agg1_scales", n)] = agg1_codes, agg1_scales
 
 
         def layer1(n):
             x_codes, x_scales = held[("x_codes", n)], held[("x_scales", n)]
-            a0_grouped = grouped.tile([P, PAIR * PACK], BF16, name="a0_grouped", tag="a0_grouped", align_bytes=64)
+            a0_grouped = held[("y_grouped", n)]
             for j in range(2):
                 a0_t = psum.tile([P, PACK, P], F32, name="a0_t%d" % j, tag="a0_t%d" % j)
                 for t in range(PACK):
@@ -221,13 +216,12 @@ def tile_graphsage_pb_t_kernel(tc, nf0, nf1, a1, w1_0, w2_0, w1_1, w2_1, out):
                     in_=a0_t[:].rearrange("p t b -> p b t"),
                     func=ACT.Relu,
                 )
-            held[("a0_grouped", n)] = a0_grouped
 
-        def quantise_hidden(n):
-            a0_codes = codes.tile([P, PAIR], U32, name="a0_codes", tag="a0_codes", align_bytes=64)
-            a0_scales = codes.tile([P, PAIR], U8, name="a0_scales", tag="a0_scales", align_bytes=64)
-            nc.vector.quantize_mx(out=a0_codes[:].bitcast(FP8X4), scales=a0_scales[:], in_=held[("a0_grouped", n)][:])
-            held[("a0_codes", n)], held[("a0_scales", n)] = a0_codes, a0_scales
+        def quantise_layer2(n):
+            y_codes = codes.tile([P, 2 * PAIR], U32, name="y_codes", tag="y_codes", align_bytes=64, bufs=2)
+            y_scales = codes.tile([P, 2 * PAIR], U8, name="y_scales", tag="y_scales", align_bytes=64, bufs=2)
+            nc.vector.quantize_mx(out=y_codes[:].bitcast(FP8X4), scales=y_scales[:], in_=held[("y_grouped", n)][:])
+            held[("y_codes", n)], held[("y_scales", n)] = y_codes, y_scales
 
         def layer2(n):
             for j in range(2):
@@ -236,12 +230,12 @@ def tile_graphsage_pb_t_kernel(tc, nf0, nf1, a1, w1_0, w2_0, w1_1, w2_1, out):
                 if place == 0:
                     held["out_bank"] = psum.tile([P, SLICES_PER_BANK, H2], F32, name="out_bank", tag="out_bank")
                 out_bank = held["out_bank"]
-                roots = slice(P * j, P * (j + 1))
-                for c, kind in enumerate(("a0", "agg1")):
+                for c in range(2):
+                    roots = slice(PAIR * c + P * j, PAIR * c + P * (j + 1))
                     nc.tensor.matmul_mx(
                         out=out_bank[:, place, :],
-                        lhsT=held[(kind + "_codes", n)][:, roots].bitcast(FP8X4),
-                        lhsT_scale=held[(kind + "_scales", n)][:, roots],
+                        lhsT=held[("y_codes", n)][:, roots].bitcast(FP8X4),
+                        lhsT_scale=held[("y_scales", n)][:, roots],
                         rhs=w_l2_codes[:, c, :].bitcast(FP8X4),
                         rhs_scale=w_l2_scales[:, c, :],
                         start=(c == 0),
@@ -252,8 +246,10 @@ def tile_graphsage_pb_t_kernel(tc, nf0, nf1, a1, w1_0, w2_0, w1_1, w2_1, out):
             if (last + 1) % count == 0:
                 first = last + 1 - count
                 result = results.tile([P, count, H2], F32, name="result", tag="result")
-                nc.vector.tensor_relu(
-                    out=result[:], in_=held["out_bank"][:, first % SLICES_PER_BANK : first % SLICES_PER_BANK + count, :]
+                nc.scalar.activation(
+                    out=result[:],
+                    in_=held["out_bank"][:, first % SLICES_PER_BANK : first % SLICES_PER_BANK + count, :],
+                    func=ACT.Relu,
                 )
                 nc.sync.dma_start(
                     out=out_rows[:, H2 * first : H2 * (first + count)], in_=result[:].rearrange("p s c -> p (s c)")
@@ -279,7 +275,7 @@ def tile_graphsage_pb_t_kernel(tc, nf0, nf1, a1, w1_0, w2_0, w1_1, w2_1, out):
             if i + AHEAD < PAIRS:
                 load_pair(i + AHEAD)
             if i >= 2:
-                quantise_hidden(i - 2)
+                quantise_layer2(i - 2)
             if i + 1 < PAIRS:
                 add_neighbours(i + 1)
                 order_roots(i + 1)

@@ -17,13 +17,19 @@ K_PASS = P * PACK
 B, D, H1, H2 = 4096, 1024, 512, 128
 FLOPS = 2 * B * (2 * D * H1 + 2 * H1 * H2)
 
-PAIRS = B // (2 * P)
-PAIR = 2 * P
+SLICES = B // P
 L1_PASSES = 2 * D // K_PASS
 NEIGHBOUR_WEIGHTS = (2, 3, L1_PASSES + 1)
 WEIGHT_ORDER = (2, 0, 3, 1)
+SINGLES = 4
+UNITS = [(x, 2) for x in range(0, SLICES - SINGLES, 2)] + [(x, 1) for x in range(SLICES - SINGLES, SLICES)]
 AHEAD = 5
 SLICES_PER_BANK = 4
+STORES = [(x, SLICES_PER_BANK) for x in range(0, SLICES - SLICES_PER_BANK, SLICES_PER_BANK)] + [
+    (SLICES - 4, 2),
+    (SLICES - 2, 1),
+    (SLICES - 1, 1),
+]
 
 
 def tile_graphsage_pb_t_kernel(tc, nf0, nf1, a1, w1_0, w2_0, w1_1, w2_1, out):
@@ -33,9 +39,9 @@ def tile_graphsage_pb_t_kernel(tc, nf0, nf1, a1, w1_0, w2_0, w1_1, w2_1, out):
         weights_in = ctx.enter_context(tc.tile_pool(name="weights_in", bufs=L1_PASSES))
         weights_grouped = ctx.enter_context(tc.tile_pool(name="weights_grouped", bufs=L1_PASSES))
         loads = ctx.enter_context(tc.tile_pool(name="loads", bufs=AHEAD + 1))
-        sums = ctx.enter_context(tc.tile_pool(name="sums", bufs=3))
+        ordered = ctx.enter_context(tc.tile_pool(name="ordered", bufs=2))
         grouped = ctx.enter_context(tc.tile_pool(name="grouped", bufs=2))
-        codes = ctx.enter_context(tc.tile_pool(name="codes", bufs=3))
+        codes = ctx.enter_context(tc.tile_pool(name="codes", bufs=2))
         results = ctx.enter_context(tc.tile_pool(name="results", bufs=4))
         psum = ctx.enter_context(tc.psum_pool(name="psum", bufs=1))
         ctx.enter_context(tc.manual_schedule())
@@ -102,193 +108,188 @@ def tile_graphsage_pb_t_kernel(tc, nf0, nf1, a1, w1_0, w2_0, w1_1, w2_1, out):
             nc.vector.quantize_mx(out=words.bitcast(FP8X4), scales=scales, in_=values)
 
 
-        def load_pair(n):
-            nf1_in = loads.tile([P, 4 * D], BF16, name="nf1_in", tag="nf1_in")
-            nc.sync.dma_start(out=nf1_in[:], in_=nf1_rows[:, 4 * D * n : 4 * D * (n + 1)])
-            a1_in = loads.tile([P, 4 * H1], BF16, name="a1_in", tag="a1_in")
-            nc.sync.dma_start(out=a1_in[:], in_=a1_rows[:, 4 * H1 * n : 4 * H1 * (n + 1)])
-            nf0_in = loads.tile([P, 2 * D], BF16, name="nf0_in", tag="nf0_in")
-            nc.sync.dma_start(out=nf0_in[:], in_=nf0_rows[:, 2 * D * n : 2 * D * (n + 1)])
-            held[("nf1", n)], held[("a1", n)], held[("nf0", n)] = nf1_in, a1_in, nf0_in
+        def load_unit(n):
+            x, count = UNITS[n]
+            for kind, rows, width in (("nf1", nf1_rows, 2 * D), ("nf0", nf0_rows, D), ("a1", a1_rows, 2 * H1)):
+                raw = loads.tile([P, count * width], BF16, name=kind + "_in", tag=kind + "_in")
+                nc.sync.dma_start(out=raw[:], in_=rows[:, width * x : width * (x + count)])
+                held[(kind, n)] = raw
 
-        def add_neighbours(n):
-            total = sums.tile([P, 2 * D + 2 * H1], BF16, name="total", tag="total")
-            for kind, width, start in (("nf1", D, 0), ("a1", H1, 2 * D)):
-                rows = held[(kind, n)][:].rearrange("p (j s w u e) -> p j s u w e", j=2, s=2, u=2, e=2)
-                for j in range(2):
-                    nc.vector.tensor_tensor(
-                        out=total[:, start + width * j : start + width * (j + 1)].rearrange(
-                            "p (u w e) -> p u w e", u=2, e=2
-                        ),
-                        in0=rows[:, j, 0],
-                        in1=rows[:, j, 1],
-                        op=ALU.add,
-                    )
-            held[("sum", n)] = total
+        def add_neighbours(n, kind, width):
+            count = UNITS[n][1]
+            total = ordered.tile([P, count * width], BF16, name=kind + "_sum", tag=kind + "_sum")
+            rows = held[(kind, n)][:].rearrange("p (j s w u e) -> p j s u w e", j=count, s=2, u=2, e=2)
+            for j in range(count):
+                nc.vector.tensor_tensor(
+                    out=total[:, width * j : width * (j + 1)].rearrange("p (u w e) -> p u w e", u=2, e=2),
+                    in0=rows[:, j, 0],
+                    in1=rows[:, j, 1],
+                    op=ALU.add,
+                )
+            held[(kind + "_words", n)] = total[:].bitcast(F32)
 
         def order_roots(n):
-            ordered = sums.tile([P, D], F32, name="ordered", tag="ordered", bufs=2)
+            count = UNITS[n][1]
+            words = ordered.tile([P, count * D // 2], F32, name="nf0_words", tag="nf0_words")
             nc.vector.tensor_copy(
-                out=ordered[:].rearrange("p (j u w) -> p j u w", j=2, u=2),
-                in_=held[("nf0", n)][:].bitcast(F32).rearrange("p (j w u) -> p j u w", j=2, u=2),
+                out=words[:].rearrange("p (j u w) -> p j u w", j=count, u=2),
+                in_=held[("nf0", n)][:].bitcast(F32).rearrange("p (j w u) -> p j u w", j=count, u=2),
             )
-            held[("ordered", n)] = ordered
+            held[("nf0_words", n)] = words
 
-        def transpose_pair(n):
-            sum_words = held[("sum", n)][:].bitcast(F32)
-            for j in range(2):
-                agg0_t = psum.tile([P, 2, 2, P], F32, name="agg0_t%d" % j, tag="agg0_t%d" % j)
-                for g in range(2):
-                    for u in range(2):
-                        w0 = (D // 2) * j + (D // 4) * u + P * g
-                        nc.tensor.transpose(agg0_t[:, g, u, :], sum_words[:, w0 : w0 + P], identity_f32[:])
-                held[("agg0_t", n, j)] = agg0_t
-            agg1_t = psum.tile([P, 2, 2, P], F32, name="agg1_t", tag="agg1_t")
-            for j in range(2):
+        def prepare(n):
+            add_neighbours(n, "nf1", D)
+            order_roots(n)
+            add_neighbours(n, "a1", H1)
+
+        def transpose_unit(n):
+            x, count = UNITS[n]
+            for kind, words in (("agg0", held[("nf1_words", n)]), ("nf0", held[("nf0_words", n)][:])):
+                for j in range(count):
+                    name = "%s_t%d" % (kind, (x + j) % 2)
+                    bank = psum.tile([P, 2, 2, P], F32, name=name, tag=name)
+                    for g in range(2):
+                        for u in range(2):
+                            w0 = (D // 2) * j + (D // 4) * u + P * g
+                            nc.tensor.transpose(bank[:, g, u, :], words[:, w0 : w0 + P], identity_f32[:])
+                    held[(kind + "_t", n, j)] = bank
+            agg1_t = psum.tile([P, count, 2, P], F32, name="agg1_t", tag="agg1_t")
+            for j in range(count):
                 for u in range(2):
-                    w0 = D + (H1 // 2) * j + P * u
-                    nc.tensor.transpose(agg1_t[:, j, u, :], sum_words[:, w0 : w0 + P], identity_f32[:])
+                    w0 = (H1 // 2) * j + P * u
+                    nc.tensor.transpose(agg1_t[:, j, u, :], held[("a1_words", n)][:, w0 : w0 + P], identity_f32[:])
             held[("agg1_t", n)] = agg1_t
-            ordered = held[("ordered", n)]
-            for j in range(2):
-                nf0_t = psum.tile([P, 2, 2, P], F32, name="nf0_t%d" % j, tag="nf0_t%d" % j)
-                for g in range(2):
-                    for u in range(2):
-                        w0 = (D // 2) * j + (D // 4) * u + P * g
-                        nc.tensor.transpose(nf0_t[:, g, u, :], ordered[:, w0 : w0 + P], identity_f32[:])
-                held[("nf0_t", n, j)] = nf0_t
 
         def copy_out(n):
-            x_grouped = grouped.tile([P, L1_PASSES * PAIR * PACK], BF16, name="x_grouped", tag="x_grouped", align_bytes=64)
-            as_words = x_grouped[:].bitcast(F32).rearrange("p (c j b u) -> p j c b u", c=L1_PASSES, j=2, b=P, u=2)
-            for j in range(2):
-                nc.scalar.copy(
-                    out=as_words[:, j, 2:4, :, :],
-                    in_=held[("agg0_t", n, j)][:].rearrange("p g u b -> p g b u"),
-                )
+            count = UNITS[n][1]
+            roots = count * P
+            x_grouped = grouped.tile(
+                [P, L1_PASSES * roots * PACK], BF16, name="x_grouped", tag="x_grouped", align_bytes=64
+            )
+            as_words = x_grouped[:].bitcast(F32).rearrange("p (c j b u) -> p j c b u", c=L1_PASSES, j=count, b=P, u=2)
+            for kind, c in (("agg0", 2), ("nf0", 0)):
+                for j in range(count):
+                    nc.scalar.copy(
+                        out=as_words[:, j, c : c + 2, :, :],
+                        in_=held[(kind + "_t", n, j)][:].rearrange("p g u b -> p g b u"),
+                    )
             y_grouped = grouped.tile(
-                [P, 2 * PAIR * PACK], BF16, name="y_grouped", tag="y_grouped", align_bytes=64, bufs=3
+                [P, 2 * roots * PACK], BF16, name="y_grouped", tag="y_grouped", align_bytes=64, bufs=3
             )
             nc.scalar.copy(
-                out=y_grouped[:, PAIR * PACK :].bitcast(F32).rearrange("p (j b u) -> p j b u", j=2, b=P, u=2),
+                out=y_grouped[:, roots * PACK :].bitcast(F32).rearrange("p (j b u) -> p j b u", j=count, b=P, u=2),
                 in_=held[("agg1_t", n)][:].rearrange("p j u b -> p j b u"),
             )
-            for j in range(2):
-                nc.scalar.copy(
-                    out=as_words[:, j, 0:2, :, :],
-                    in_=held[("nf0_t", n, j)][:].rearrange("p g u b -> p g b u"),
-                )
             held[("x_grouped", n)], held[("y_grouped", n)] = x_grouped, y_grouped
 
-        def quantise_pair(n):
-            x_codes = codes.tile([P, L1_PASSES * PAIR], U32, name="x_codes", tag="x_codes", align_bytes=64)
-            x_scales = codes.tile([P, L1_PASSES * PAIR], U8, name="x_scales", tag="x_scales", align_bytes=64)
+        def quantise_layer1(n):
+            roots = UNITS[n][1] * P
+            x_codes = codes.tile([P, L1_PASSES * roots], U32, name="x_codes", tag="x_codes", align_bytes=64)
+            x_scales = codes.tile([P, L1_PASSES * roots], U8, name="x_scales", tag="x_scales", align_bytes=64)
             for half in (1, 0):
-                cols = slice(2 * PAIR * half, 2 * PAIR * (half + 1))
+                cols = slice(2 * roots * half, 2 * roots * (half + 1))
                 nc.vector.quantize_mx(
                     out=x_codes[:, cols].bitcast(FP8X4),
                     scales=x_scales[:, cols],
-                    in_=held[("x_grouped", n)][:, 2 * PAIR * PACK * half : 2 * PAIR * PACK * (half + 1)],
+                    in_=held[("x_grouped", n)][:, 2 * roots * PACK * half : 2 * roots * PACK * (half + 1)],
                 )
             held[("x_codes", n)], held[("x_scales", n)] = x_codes, x_scales
 
 
         def layer1(n):
+            x, count = UNITS[n]
+            roots = count * P
             x_codes, x_scales = held[("x_codes", n)], held[("x_scales", n)]
-            a0_grouped = held[("y_grouped", n)]
-            for j in range(2):
-                a0_t = psum.tile([P, PACK, P], F32, name="a0_t%d" % j, tag="a0_t%d" % j)
-                for t in range(PACK):
-                    hidden = slice(P * t, P * (t + 1))
+            tiles = PACK // count
+            by_bank = held[("y_grouped", n)][:, 0 : roots * PACK].rearrange("p (b h t) -> p h b t", h=count, t=tiles)
+            for h in range(count):
+                name = "a0_t%d" % ((x + h) % 2)
+                a0_t = psum.tile([P, tiles, roots], F32, name=name, tag=name)
+                for t in range(tiles):
+                    hidden = slice(P * (tiles * h + t), P * (tiles * h + t + 1))
                     for c in range(L1_PASSES):
-                        roots = slice(PAIR * c + P * j, PAIR * c + P * (j + 1))
+                        cols = slice(roots * c, roots * (c + 1))
                         nc.tensor.matmul_mx(
                             out=a0_t[:, t, :],
                             lhsT=w_l1_codes[:, c, hidden].bitcast(FP8X4),
                             lhsT_scale=w_l1_scales[:, c, hidden],
-                            rhs=x_codes[:, roots].bitcast(FP8X4),
-                            rhs_scale=x_scales[:, roots],
+                            rhs=x_codes[:, cols].bitcast(FP8X4),
+                            rhs_scale=x_scales[:, cols],
                             start=(c == 0),
                             stop=(c == L1_PASSES - 1),
                         )
-                nc.scalar.activation(
-                    out=a0_grouped[:, P * PACK * j : P * PACK * (j + 1)].rearrange("p (b t) -> p b t", t=PACK),
-                    in_=a0_t[:].rearrange("p t b -> p b t"),
-                    func=ACT.Relu,
-                )
+                nc.scalar.activation(out=by_bank[:, h, :, :], in_=a0_t[:].rearrange("p t b -> p b t"), func=ACT.Relu)
 
         def quantise_layer2(n):
-            y_codes = codes.tile([P, 2 * PAIR], U32, name="y_codes", tag="y_codes", align_bytes=64, bufs=2)
-            y_scales = codes.tile([P, 2 * PAIR], U8, name="y_scales", tag="y_scales", align_bytes=64, bufs=2)
+            roots = UNITS[n][1] * P
+            y_codes = codes.tile([P, 2 * roots], U32, name="y_codes", tag="y_codes", align_bytes=64)
+            y_scales = codes.tile([P, 2 * roots], U8, name="y_scales", tag="y_scales", align_bytes=64)
             nc.vector.quantize_mx(out=y_codes[:].bitcast(FP8X4), scales=y_scales[:], in_=held[("y_grouped", n)][:])
             held[("y_codes", n)], held[("y_scales", n)] = y_codes, y_scales
 
         def layer2(n):
-            for j in range(2):
-                x = 2 * n + j
-                place = x % SLICES_PER_BANK
+            first, count = UNITS[n]
+            for j in range(count):
+                place = (first + j) % SLICES_PER_BANK
                 if place == 0:
                     held["out_bank"] = psum.tile([P, SLICES_PER_BANK, H2], F32, name="out_bank", tag="out_bank")
-                out_bank = held["out_bank"]
                 for c in range(2):
-                    roots = slice(PAIR * c + P * j, PAIR * c + P * (j + 1))
+                    cols = slice(P * (count * c + j), P * (count * c + j + 1))
                     nc.tensor.matmul_mx(
-                        out=out_bank[:, place, :],
-                        lhsT=held[("y_codes", n)][:, roots].bitcast(FP8X4),
-                        lhsT_scale=held[("y_scales", n)][:, roots],
+                        out=held["out_bank"][:, place, :],
+                        lhsT=held[("y_codes", n)][:, cols].bitcast(FP8X4),
+                        lhsT_scale=held[("y_scales", n)][:, cols],
                         rhs=w_l2_codes[:, c, :].bitcast(FP8X4),
                         rhs_scale=w_l2_scales[:, c, :],
                         start=(c == 0),
                         stop=(c == 1),
                     )
-            count = 2 if n >= PAIRS - 2 else SLICES_PER_BANK
-            last = 2 * n + 1
-            if (last + 1) % count == 0:
-                first = last + 1 - count
-                result = results.tile([P, count, H2], F32, name="result", tag="result")
-                nc.scalar.activation(
-                    out=result[:],
-                    in_=held["out_bank"][:, first % SLICES_PER_BANK : first % SLICES_PER_BANK + count, :],
-                    func=ACT.Relu,
-                )
-                nc.sync.dma_start(
-                    out=out_rows[:, H2 * first : H2 * (first + count)], in_=result[:].rearrange("p s c -> p (s c)")
-                )
+
+        def store_out(n):
+            x, units_slices = UNITS[n]
+            for first, count in STORES:
+                if first + count == x + units_slices:
+                    place = first % SLICES_PER_BANK
+                    result = results.tile([P, count, H2], F32, name="result", tag="result")
+                    nc.vector.tensor_relu(out=result[:], in_=held["out_bank"][:, place : place + count, :])
+                    nc.sync.dma_start(
+                        out=out_rows[:, H2 * first : H2 * (first + count)], in_=result[:].rearrange("p s c -> p (s c)")
+                    )
 
 
         load_layer1_weights()
-        load_pair(0)
-        load_pair(1)
+        load_unit(0)
+        load_unit(1)
         load_layer2_weights()
         for n in range(2, AHEAD):
-            load_pair(n)
+            load_unit(n)
 
         for c in WEIGHT_ORDER:
             group_weights(c)
         for c in WEIGHT_ORDER[:-1]:
             quantise_weights(c)
-        add_neighbours(0)
-        order_roots(0)
+        prepare(0)
         quantise_weights(WEIGHT_ORDER[-1])
 
-        for i in range(PAIRS + 2):
-            if i + AHEAD < PAIRS:
-                load_pair(i + AHEAD)
+        last = len(UNITS)
+        for i in range(last + 2):
+            if i + AHEAD < last:
+                load_unit(i + AHEAD)
             if i >= 2:
                 quantise_layer2(i - 2)
-            if i + 1 < PAIRS:
-                add_neighbours(i + 1)
-                order_roots(i + 1)
-            if i < PAIRS:
-                transpose_pair(i)
+            if i + 1 < last:
+                prepare(i + 1)
+            if i < last:
+                transpose_unit(i)
                 copy_out(i)
-                quantise_pair(i)
+                quantise_layer1(i)
             if i == 0:
-                group_weights(4)
-                group_weights(5)
-                quantise_weights(4)
-                quantise_weights(5)
-            if 1 <= i <= PAIRS:
+                for c in (L1_PASSES, L1_PASSES + 1):
+                    group_weights(c)
+                for c in (L1_PASSES, L1_PASSES + 1):
+                    quantise_weights(c)
+            if 1 <= i <= last:
                 layer1(i - 1)
             if i >= 2:
                 layer2(i - 2)
+                store_out(i - 2)

@@ -21,7 +21,7 @@ SLICES = B // P
 L1_PASSES = 2 * D // K_PASS
 NEIGHBOUR_WEIGHTS = (2, 3, L1_PASSES + 1)
 WEIGHT_ORDER = (2, 0, 3, 1)
-SINGLES = 4
+SINGLES = 2
 UNITS = [(x, 2) for x in range(0, SLICES - SINGLES, 2)] + [(x, 1) for x in range(SLICES - SINGLES, SLICES)]
 AHEAD = 5
 SLICES_PER_BANK = 4
@@ -39,7 +39,7 @@ def tile_graphsage_pb_t_kernel(tc, nf0, nf1, a1, w1_0, w2_0, w1_1, w2_1, out):
         weights_in = ctx.enter_context(tc.tile_pool(name="weights_in", bufs=L1_PASSES))
         weights_grouped = ctx.enter_context(tc.tile_pool(name="weights_grouped", bufs=L1_PASSES))
         loads = ctx.enter_context(tc.tile_pool(name="loads", bufs=AHEAD + 1))
-        ordered = ctx.enter_context(tc.tile_pool(name="ordered", bufs=2))
+        ordered = ctx.enter_context(tc.tile_pool(name="ordered", bufs=3))
         grouped = ctx.enter_context(tc.tile_pool(name="grouped", bufs=2))
         codes = ctx.enter_context(tc.tile_pool(name="codes", bufs=2))
         results = ctx.enter_context(tc.tile_pool(name="results", bufs=4))
@@ -137,12 +137,7 @@ def tile_graphsage_pb_t_kernel(tc, nf0, nf1, a1, w1_0, w2_0, w1_1, w2_1, out):
             )
             held[("nf0_words", n)] = words
 
-        def prepare(n):
-            add_neighbours(n, "nf1", D)
-            order_roots(n)
-            add_neighbours(n, "a1", H1)
-
-        def transpose_unit(n):
+        def transpose_layer1(n):
             x, count = UNITS[n]
             for kind, words in (("agg0", held[("nf1_words", n)]), ("nf0", held[("nf0_words", n)][:])):
                 for j in range(count):
@@ -153,6 +148,9 @@ def tile_graphsage_pb_t_kernel(tc, nf0, nf1, a1, w1_0, w2_0, w1_1, w2_1, out):
                             w0 = (D // 2) * j + (D // 4) * u + P * g
                             nc.tensor.transpose(bank[:, g, u, :], words[:, w0 : w0 + P], identity_f32[:])
                     held[(kind + "_t", n, j)] = bank
+
+        def transpose_layer2(n):
+            count = UNITS[n][1]
             agg1_t = psum.tile([P, count, 2, P], F32, name="agg1_t", tag="agg1_t")
             for j in range(count):
                 for u in range(2):
@@ -160,7 +158,7 @@ def tile_graphsage_pb_t_kernel(tc, nf0, nf1, a1, w1_0, w2_0, w1_1, w2_1, out):
                     nc.tensor.transpose(agg1_t[:, j, u, :], held[("a1_words", n)][:, w0 : w0 + P], identity_f32[:])
             held[("agg1_t", n)] = agg1_t
 
-        def copy_out(n):
+        def copy_layer1(n):
             count = UNITS[n][1]
             roots = count * P
             x_grouped = grouped.tile(
@@ -173,14 +171,17 @@ def tile_graphsage_pb_t_kernel(tc, nf0, nf1, a1, w1_0, w2_0, w1_1, w2_1, out):
                         out=as_words[:, j, c : c + 2, :, :],
                         in_=held[(kind + "_t", n, j)][:].rearrange("p g u b -> p g b u"),
                     )
-            y_grouped = grouped.tile(
-                [P, 2 * roots * PACK], BF16, name="y_grouped", tag="y_grouped", align_bytes=64, bufs=3
-            )
+            held[("x_grouped", n)] = x_grouped
+
+        def copy_layer2(n):
+            count = UNITS[n][1]
+            roots = count * P
+            y_grouped = grouped.tile([P, 2 * roots * PACK], BF16, name="y_grouped", tag="y_grouped", align_bytes=64)
             nc.scalar.copy(
                 out=y_grouped[:, roots * PACK :].bitcast(F32).rearrange("p (j b u) -> p j b u", j=count, b=P, u=2),
                 in_=held[("agg1_t", n)][:].rearrange("p j u b -> p j b u"),
             )
-            held[("x_grouped", n)], held[("y_grouped", n)] = x_grouped, y_grouped
+            held[("y_grouped", n)] = y_grouped
 
         def quantise_layer1(n):
             roots = UNITS[n][1] * P
@@ -268,8 +269,10 @@ def tile_graphsage_pb_t_kernel(tc, nf0, nf1, a1, w1_0, w2_0, w1_1, w2_1, out):
             group_weights(c)
         for c in WEIGHT_ORDER[:-1]:
             quantise_weights(c)
-        prepare(0)
+        add_neighbours(0, "nf1", D)
+        order_roots(0)
         quantise_weights(WEIGHT_ORDER[-1])
+        add_neighbours(0, "a1", H1)
 
         last = len(UNITS)
         for i in range(last + 2):
@@ -278,11 +281,20 @@ def tile_graphsage_pb_t_kernel(tc, nf0, nf1, a1, w1_0, w2_0, w1_1, w2_1, out):
             if i >= 2:
                 quantise_layer2(i - 2)
             if i + 1 < last:
-                prepare(i + 1)
+                add_neighbours(i + 1, "nf1", D)
+                order_roots(i + 1)
             if i < last:
-                transpose_unit(i)
-                copy_out(i)
+                transpose_layer1(i)
+            if 1 <= i <= last:
+                transpose_layer2(i - 1)
+            if i < last:
+                copy_layer1(i)
+            if 1 <= i <= last:
+                copy_layer2(i - 1)
+            if i < last:
                 quantise_layer1(i)
+            if i + 1 < last:
+                add_neighbours(i + 1, "a1", H1)
             if i == 0:
                 for c in (L1_PASSES, L1_PASSES + 1):
                     group_weights(c)

@@ -25,11 +25,13 @@ SINGLES = 2
 UNITS = [(x, 2) for x in range(0, SLICES - SINGLES, 2)] + [(x, 1) for x in range(SLICES - SINGLES, SLICES)]
 AHEAD = 5
 SLICES_PER_BANK = 4
-STORES = [(x, SLICES_PER_BANK) for x in range(0, SLICES - SLICES_PER_BANK, SLICES_PER_BANK)] + [
+RELUS = [(x, SLICES_PER_BANK) for x in range(0, SLICES - SLICES_PER_BANK, SLICES_PER_BANK)] + [
     (SLICES - 4, 2),
     (SLICES - 2, 1),
     (SLICES - 1, 1),
 ]
+EARLY_SLICES = sum(count for first, count in UNITS[: len(UNITS) - AHEAD - 2])
+STORES = [(0, EARLY_SLICES)] + [(first, count) for first, count in RELUS if first >= EARLY_SLICES]
 
 
 def tile_graphsage_pb_t_kernel(tc, nf0, nf1, a1, w1_0, w2_0, w1_1, w2_1, out):
@@ -42,7 +44,6 @@ def tile_graphsage_pb_t_kernel(tc, nf0, nf1, a1, w1_0, w2_0, w1_1, w2_1, out):
         ordered = ctx.enter_context(tc.tile_pool(name="ordered", bufs=3))
         grouped = ctx.enter_context(tc.tile_pool(name="grouped", bufs=2))
         codes = ctx.enter_context(tc.tile_pool(name="codes", bufs=2))
-        results = ctx.enter_context(tc.tile_pool(name="results", bufs=4))
         psum = ctx.enter_context(tc.psum_pool(name="psum", bufs=1))
         ctx.enter_context(tc.manual_schedule())
 
@@ -58,6 +59,8 @@ def tile_graphsage_pb_t_kernel(tc, nf0, nf1, a1, w1_0, w2_0, w1_1, w2_1, out):
         w_l1_scales = const.tile([P, L1_PASSES, H1], U8, name="w_l1_scales", align_bytes=64)
         w_l2_codes = const.tile([P, 2, H2], U32, name="w_l2_codes", align_bytes=64)
         w_l2_scales = const.tile([P, 2, H2], U8, name="w_l2_scales", align_bytes=64)
+
+        results = const.tile([P, SLICES, H2], F32, name="results")
 
         held = {}
 
@@ -247,14 +250,17 @@ def tile_graphsage_pb_t_kernel(tc, nf0, nf1, a1, w1_0, w2_0, w1_1, w2_1, out):
                     )
 
         def store_out(n):
-            x, units_slices = UNITS[n]
-            for first, count in STORES:
-                if first + count == x + units_slices:
+            end = sum(UNITS[n])
+            for first, count in RELUS:
+                if first + count == end:
                     place = first % SLICES_PER_BANK
-                    result = results.tile([P, count, H2], F32, name="result", tag="result")
-                    nc.vector.tensor_relu(out=result[:], in_=held["out_bank"][:, place : place + count, :])
+                    nc.vector.tensor_relu(
+                        out=results[:, first:end, :], in_=held["out_bank"][:, place : place + count, :]
+                    )
+            for first, count in STORES:
+                if first + count == end:
                     nc.sync.dma_start(
-                        out=out_rows[:, H2 * first : H2 * (first + count)], in_=result[:].rearrange("p s c -> p (s c)")
+                        out=out_rows[:, H2 * first : H2 * end], in_=results[:, first:end, :].rearrange("p s c -> p (s c)")
                     )
 
 

@@ -55,10 +55,15 @@ def tile_graphsage_pb_t_kernel(tc, nf0, nf1, a1, w1_0, w2_0, w1_1, w2_1, out):
         identity_f32 = const.tile([P, P], F32, name="identity_f32")
         make_identity(nc, identity_f32[:])
 
-        w_l1_codes = const.tile([P, L1_PASSES, H1], U32, name="w_l1_codes", align_bytes=64)
-        w_l1_scales = const.tile([P, L1_PASSES, H1], U8, name="w_l1_scales", align_bytes=64)
-        w_l2_codes = const.tile([P, 2, H2], U32, name="w_l2_codes", align_bytes=64)
-        w_l2_scales = const.tile([P, 2, H2], U8, name="w_l2_scales", align_bytes=64)
+        def quarter(pool, q, width, dtype, name):
+            pad = 64 * q // (4 if dtype == U32 else 1)
+            tile = pool.tile([P, pad + width], dtype, name=name, tag=name, align_bytes=256)
+            return tile[:, pad:]
+
+        w_l1_codes = quarter(const, 2, L1_PASSES * H1, U32, "w_l1_codes").rearrange("p (c h) -> p c h", c=L1_PASSES)
+        w_l1_scales = quarter(const, 3, L1_PASSES * H1, U8, "w_l1_scales").rearrange("p (c h) -> p c h", c=L1_PASSES)
+        w_l2_codes = quarter(const, 2, 2 * H2, U32, "w_l2_codes").rearrange("p (c h) -> p c h", c=2)
+        w_l2_scales = quarter(const, 3, 2 * H2, U8, "w_l2_scales").rearrange("p (c h) -> p c h", c=2)
 
         results = const.tile([P, SLICES, H2], F32, name="results")
 
@@ -188,8 +193,8 @@ def tile_graphsage_pb_t_kernel(tc, nf0, nf1, a1, w1_0, w2_0, w1_1, w2_1, out):
 
         def quantise_layer1(n):
             roots = UNITS[n][1] * P
-            x_codes = codes.tile([P, L1_PASSES * roots], U32, name="x_codes", tag="x_codes", align_bytes=64)
-            x_scales = codes.tile([P, L1_PASSES * roots], U8, name="x_scales", tag="x_scales", align_bytes=64)
+            x_codes = quarter(codes, 0, L1_PASSES * roots, U32, "x_codes")
+            x_scales = quarter(codes, 1, L1_PASSES * roots, U8, "x_scales")
             for half in (1, 0):
                 cols = slice(2 * roots * half, 2 * roots * (half + 1))
                 nc.vector.quantize_mx(
@@ -226,9 +231,9 @@ def tile_graphsage_pb_t_kernel(tc, nf0, nf1, a1, w1_0, w2_0, w1_1, w2_1, out):
 
         def quantise_layer2(n):
             roots = UNITS[n][1] * P
-            y_codes = codes.tile([P, 2 * roots], U32, name="y_codes", tag="y_codes", align_bytes=64)
-            y_scales = codes.tile([P, 2 * roots], U8, name="y_scales", tag="y_scales", align_bytes=64)
-            nc.vector.quantize_mx(out=y_codes[:].bitcast(FP8X4), scales=y_scales[:], in_=held[("y_grouped", n)][:])
+            y_codes = quarter(codes, 0, 2 * roots, U32, "y_codes")
+            y_scales = quarter(codes, 1, 2 * roots, U8, "y_scales")
+            nc.vector.quantize_mx(out=y_codes.bitcast(FP8X4), scales=y_scales, in_=held[("y_grouped", n)][:])
             held[("y_codes", n)], held[("y_scales", n)] = y_codes, y_scales
 
         def layer2(n):

from contextlib import ExitStack

import concourse.mybir as mybir
from concourse.masks import make_identity

F32 = mybir.dt.float32
BF16 = mybir.dt.bfloat16
U32 = mybir.dt.uint32
U8 = mybir.dt.uint8
FP8X4 = mybir.dt.float8_e4m3fn_x4
ACT = mybir.ActivationFunctionType
ALU = mybir.AluOpType

P = 128
PACK = 4
K_PASS = P * PACK
B, D, H1, H2 = 4096, 1024, 512, 128
FLOPS = 2 * B * (2 * D * H1 + 2 * H1 * H2)

SLICES = B // P
L1_PASSES = 2 * D // K_PASS
NEIGHBOUR_WEIGHTS = (2, 3, L1_PASSES + 1)
WEIGHT_ORDER = (2, 0, 3, 1)
SINGLES = 2
UNITS = [(x, 2) for x in range(0, SLICES - SINGLES, 2)] + [(x, 1) for x in range(SLICES - SINGLES, SLICES)]
AHEAD = 5
SLICES_PER_BANK = 4
RELUS = [(x, SLICES_PER_BANK) for x in range(0, SLICES - SLICES_PER_BANK, SLICES_PER_BANK)] + [
    (SLICES - 4, 2),
    (SLICES - 2, 1),
    (SLICES - 1, 1),
]
EARLY_SLICES = sum(count for first, count in UNITS[: len(UNITS) - AHEAD - 2])
STORES = [(0, EARLY_SLICES)] + [(first, count) for first, count in RELUS if first >= EARLY_SLICES]


def tile_graphsage_pb_t_kernel(tc, nf0, nf1, a1, w1_0, w2_0, w1_1, w2_1, out):
    nc = tc.nc
    with ExitStack() as ctx:
        const = ctx.enter_context(tc.tile_pool(name="const", bufs=1))
        weights_in = ctx.enter_context(tc.tile_pool(name="weights_in", bufs=L1_PASSES))
        weights_grouped = ctx.enter_context(tc.tile_pool(name="weights_grouped", bufs=L1_PASSES))
        loads = ctx.enter_context(tc.tile_pool(name="loads", bufs=AHEAD + 1))
        ordered = ctx.enter_context(tc.tile_pool(name="ordered", bufs=3))
        grouped = ctx.enter_context(tc.tile_pool(name="grouped", bufs=2))
        codes = ctx.enter_context(tc.tile_pool(name="codes", bufs=2))
        psum = ctx.enter_context(tc.psum_pool(name="psum", bufs=1))
        ctx.enter_context(tc.manual_schedule())

        nf0_rows = nf0.rearrange("(p x) k -> p (x k)", p=P)
        nf1_rows = nf1.rearrange("(p x) k -> p (x k)", p=P)
        a1_rows = a1.rearrange("(p x) k -> p (x k)", p=P)
        out_rows = out.rearrange("(p x) c -> p (x c)", p=P)

        identity_f32 = const.tile([P, P], F32, name="identity_f32")
        make_identity(nc, identity_f32[:])

        def quarter(pool, q, width, dtype, name):
            pad = 64 * q // (4 if dtype == U32 else 1)
            tile = pool.tile([P, pad + width], dtype, name=name, tag=name, align_bytes=256)
            return tile[:, pad:]

        w_l1_codes = quarter(const, 2, L1_PASSES * H1, U32, "w_l1_codes").rearrange("p (c h) -> p c h", c=L1_PASSES)
        w_l1_scales = quarter(const, 3, L1_PASSES * H1, U8, "w_l1_scales").rearrange("p (c h) -> p c h", c=L1_PASSES)
        w_l2_codes = quarter(const, 2, 2 * H2, U32, "w_l2_codes").rearrange("p (c h) -> p c h", c=2)
        w_l2_scales = quarter(const, 3, 2 * H2, U8, "w_l2_scales").rearrange("p (c h) -> p c h", c=2)

        results = const.tile([P, SLICES, H2], F32, name="results")

        held = {}


        def load_layer1_weights():
            for c in WEIGHT_ORDER:
                raw = weights_in.tile([P, PACK, H1], BF16, name="w_l1_raw", tag="w_l1_raw")
                w = w2_0 if c < 2 else w1_0
                rows = w[K_PASS * (c % 2) : K_PASS * (c % 2 + 1), :]
                nc.sync.dma_start(out=raw[:], in_=rows.rearrange("(p t) h -> p t h", t=PACK))
                held[("w_raw", c)] = raw

        def load_layer2_weights():
            for c, w in enumerate((w2_1, w1_1)):
                raw = weights_in.tile([P, PACK, H2], BF16, name="w_l2_raw", tag="w_l2_raw", bufs=2)
                nc.sync.dma_start(out=raw[:], in_=w.rearrange("(p t) c -> p t c", t=PACK))
                held[("w_raw", L1_PASSES + c)] = raw

        def group_weights(c):
            if c in NEIGHBOUR_WEIGHTS:
                engine_copy = lambda out, in_: nc.vector.tensor_scalar_mul(out=out, in0=in_, scalar1=0.5)
            elif c < L1_PASSES:
                engine_copy = nc.scalar.copy
            else:
                engine_copy = nc.vector.tensor_copy
            width = H1 if c < L1_PASSES else H2
            side_by_side = weights_grouped.tile(
                [P, width, PACK], BF16, name="w_grouped", tag="w_grouped_%d" % width, align_bytes=64
            )
            if c < L1_PASSES:
                engine_copy(
                    out=side_by_side[:].rearrange("p (q m) t -> p q m t", q=PACK),
                    in_=held[("w_raw", c)][:].rearrange("p t (m q) -> p q m t", q=PACK),
                )
            else:
                engine_copy(
                    out=side_by_side[:].rearrange("p (c i) t -> p c t i", i=4),
                    in_=held[("w_raw", c)][:].rearrange("p t (c i) -> p c t i", i=4),
                )
            held[("w_grouped", c)] = side_by_side

        def quantise_weights(c):
            values = held[("w_grouped", c)][:].rearrange("p h t -> p (h t)")
            if c < L1_PASSES:
                words, scales = w_l1_codes[:, c, :], w_l1_scales[:, c, :]
            else:
                words, scales = w_l2_codes[:, c - L1_PASSES, :], w_l2_scales[:, c - L1_PASSES, :]
            nc.vector.quantize_mx(out=words.bitcast(FP8X4), scales=scales, in_=values)


        def load_unit(n):
            x, count = UNITS[n]
            for kind, rows, width in (("nf1", nf1_rows, 2 * D), ("nf0", nf0_rows, D), ("a1", a1_rows, 2 * H1)):
                raw = loads.tile([P, count * width], BF16, name=kind + "_in", tag=kind + "_in")
                nc.sync.dma_start(out=raw[:], in_=rows[:, width * x : width * (x + count)])
                held[(kind, n)] = raw

        def add_neighbours(n, kind, width):
            count = UNITS[n][1]
            total = ordered.tile([P, count * width], BF16, name=kind + "_sum", tag=kind + "_sum")
            rows = held[(kind, n)][:].rearrange("p (j s w u e) -> p j s u w e", j=count, s=2, u=2, e=2)
            for j in range(count):
                nc.vector.tensor_tensor(
                    out=total[:, width * j : width * (j + 1)].rearrange("p (u w e) -> p u w e", u=2, e=2),
                    in0=rows[:, j, 0],
                    in1=rows[:, j, 1],
                    op=ALU.add,
                )
            held[(kind + "_words", n)] = total[:].bitcast(F32)

        def order_roots(n):
            count = UNITS[n][1]
            words = ordered.tile([P, count * D // 2], F32, name="nf0_words", tag="nf0_words")
            nc.vector.tensor_copy(
                out=words[:].rearrange("p (j u w) -> p j u w", j=count, u=2),
                in_=held[("nf0", n)][:].bitcast(F32).rearrange("p (j w u) -> p j u w", j=count, u=2),
            )
            held[("nf0_words", n)] = words

        def transpose_layer1(n):
            x, count = UNITS[n]
            for kind, words in (("agg0", held[("nf1_words", n)]), ("nf0", held[("nf0_words", n)][:])):
                for j in range(count):
                    name = "%s_t%d" % (kind, (x + j) % 2)
                    bank = psum.tile([P, 2, 2, P], F32, name=name, tag=name)
                    for g in range(2):
                        for u in range(2):
                            w0 = (D // 2) * j + (D // 4) * u + P * g
                            nc.tensor.transpose(bank[:, g, u, :], words[:, w0 : w0 + P], identity_f32[:])
                    held[(kind + "_t", n, j)] = bank

        def transpose_layer2(n):
            count = UNITS[n][1]
            agg1_t = psum.tile([P, count, 2, P], F32, name="agg1_t", tag="agg1_t")
            for j in range(count):
                for u in range(2):
                    w0 = (H1 // 2) * j + P * u
                    nc.tensor.transpose(agg1_t[:, j, u, :], held[("a1_words", n)][:, w0 : w0 + P], identity_f32[:])
            held[("agg1_t", n)] = agg1_t

        def copy_layer1(n):
            count = UNITS[n][1]
            roots = count * P
            x_grouped = grouped.tile(
                [P, L1_PASSES * roots * PACK], BF16, name="x_grouped", tag="x_grouped", align_bytes=64
            )
            as_words = x_grouped[:].bitcast(F32).rearrange("p (c j b u) -> p j c b u", c=L1_PASSES, j=count, b=P, u=2)
            for kind, c in (("agg0", 2), ("nf0", 0)):
                for j in range(count):
                    nc.scalar.copy(
                        out=as_words[:, j, c : c + 2, :, :],
                        in_=held[(kind + "_t", n, j)][:].rearrange("p g u b -> p g b u"),
                    )
            held[("x_grouped", n)] = x_grouped

        def copy_layer2(n):
            count = UNITS[n][1]
            roots = count * P
            y_grouped = grouped.tile([P, 2 * roots * PACK], BF16, name="y_grouped", tag="y_grouped", align_bytes=64)
            nc.scalar.copy(
                out=y_grouped[:, roots * PACK :].bitcast(F32).rearrange("p (j b u) -> p j b u", j=count, b=P, u=2),
                in_=held[("agg1_t", n)][:].rearrange("p j u b -> p j b u"),
            )
            held[("y_grouped", n)] = y_grouped

        def quantise_layer1(n):
            roots = UNITS[n][1] * P
            x_codes = quarter(codes, 0, L1_PASSES * roots, U32, "x_codes")
            x_scales = quarter(codes, 1, L1_PASSES * roots, U8, "x_scales")
            for half in (1, 0):
                cols = slice(2 * roots * half, 2 * roots * (half + 1))
                nc.vector.quantize_mx(
                    out=x_codes[:, cols].bitcast(FP8X4),
                    scales=x_scales[:, cols],
                    in_=held[("x_grouped", n)][:, 2 * roots * PACK * half : 2 * roots * PACK * (half + 1)],
                )
            held[("x_codes", n)], held[("x_scales", n)] = x_codes, x_scales


        def layer1(n):
            x, count = UNITS[n]
            roots = count * P
            x_codes, x_scales = held[("x_codes", n)], held[("x_scales", n)]
            tiles = PACK // count
            by_bank = held[("y_grouped", n)][:, 0 : roots * PACK].rearrange("p (b h t) -> p h b t", h=count, t=tiles)
            for h in range(count):
                name = "a0_t%d" % ((x + h) % 2)
                a0_t = psum.tile([P, tiles, roots], F32, name=name, tag=name)
                for t in range(tiles):
                    hidden = slice(P * (tiles * h + t), P * (tiles * h + t + 1))
                    for c in range(L1_PASSES):
                        cols = slice(roots * c, roots * (c + 1))
                        nc.tensor.matmul_mx(
                            out=a0_t[:, t, :],
                            lhsT=w_l1_codes[:, c, hidden].bitcast(FP8X4),
                            lhsT_scale=w_l1_scales[:, c, hidden],
                            rhs=x_codes[:, cols].bitcast(FP8X4),
                            rhs_scale=x_scales[:, cols],
                            start=(c == 0),
                            stop=(c == L1_PASSES - 1),
                        )
                nc.scalar.activation(out=by_bank[:, h, :, :], in_=a0_t[:].rearrange("p t b -> p b t"), func=ACT.Relu)

        def quantise_layer2(n):
            roots = UNITS[n][1] * P
            y_codes = quarter(codes, 0, 2 * roots, U32, "y_codes")
            y_scales = quarter(codes, 1, 2 * roots, U8, "y_scales")
            nc.vector.quantize_mx(out=y_codes.bitcast(FP8X4), scales=y_scales, in_=held[("y_grouped", n)][:])
            held[("y_codes", n)], held[("y_scales", n)] = y_codes, y_scales

        def layer2(n):
            first, count = UNITS[n]
            for j in range(count):
                place = (first + j) % SLICES_PER_BANK
                if place == 0:
                    held["out_bank"] = psum.tile([P, SLICES_PER_BANK, H2], F32, name="out_bank", tag="out_bank")
                for c in range(2):
                    cols = slice(P * (count * c + j), P * (count * c + j + 1))
                    nc.tensor.matmul_mx(
                        out=held["out_bank"][:, place, :],
                        lhsT=held[("y_codes", n)][:, cols].bitcast(FP8X4),
                        lhsT_scale=held[("y_scales", n)][:, cols],
                        rhs=w_l2_codes[:, c, :].bitcast(FP8X4),
                        rhs_scale=w_l2_scales[:, c, :],
                        start=(c == 0),
                        stop=(c == 1),
                    )

        def store_out(n):
            end = sum(UNITS[n])
            for first, count in RELUS:
                if first + count == end:
                    place = first % SLICES_PER_BANK
                    nc.vector.tensor_relu(
                        out=results[:, first:end, :], in_=held["out_bank"][:, place : place + count, :]
                    )
            for first, count in STORES:
                if first + count == end:
                    nc.sync.dma_start(
                        out=out_rows[:, H2 * first : H2 * end], in_=results[:, first:end, :].rearrange("p s c -> p (s c)")
                    )


        load_layer1_weights()
        load_unit(0)
        load_unit(1)
        load_layer2_weights()
        for n in range(2, AHEAD):
            load_unit(n)

        for c in WEIGHT_ORDER:
            group_weights(c)
        for c in WEIGHT_ORDER[:-1]:
            quantise_weights(c)
        add_neighbours(0, "nf1", D)
        order_roots(0)
        quantise_weights(WEIGHT_ORDER[-1])
        add_neighbours(0, "a1", H1)

        last = len(UNITS)
        for i in range(last + 2):
            if i + AHEAD < last:
                load_unit(i + AHEAD)
            if i >= 2:
                quantise_layer2(i - 2)
            if i + 1 < last:
                add_neighbours(i + 1, "nf1", D)
                order_roots(i + 1)
            if i < last:
                transpose_layer1(i)
            if 1 <= i <= last:
                transpose_layer2(i - 1)
            if i < last:
                copy_layer1(i)
            if 1 <= i <= last:
                copy_layer2(i - 1)
            if i < last:
                quantise_layer1(i)
            if i + 1 < last:
                add_neighbours(i + 1, "a1", H1)
            if i == 0:
                for c in (L1_PASSES, L1_PASSES + 1):
                    group_weights(c)
                for c in (L1_PASSES, L1_PASSES + 1):
                    quantise_weights(c)
            if 1 <= i <= last:
                layer1(i - 1)
            if i >= 2:
                layer2(i - 2)
                store_out(i - 2)
